import numpy as np
import ml_dtypes


def mxq(x, axis, fmt="e4m3"):
    dtype, down = {"e4m3": (ml_dtypes.float8_e4m3fn, 7), "e5m2": (ml_dtypes.float8_e5m2, 14)}[fmt]
    v = np.moveaxis(np.asarray(x, np.float32).astype(ml_dtypes.bfloat16).astype(np.float64), axis, -1)
    blocks = v.reshape(v.shape[:-1] + (-1, 32))
    amax = np.abs(blocks).max(-1, keepdims=True)
    byte = np.maximum(np.where(amax > 0, np.frexp(amax)[1] - 1 + 127, 0) - down, 1)
    scale = np.exp2(byte - 127.0)
    codes = (blocks / scale).astype(np.float32).astype(dtype).astype(np.float64)
    return np.moveaxis((codes * scale).reshape(v.shape), -1, axis)


WIDE = False


def mx_kscale(k):
    if not WIDE:
        return np.ones(k)
    levels = np.array([10, -10, 5, -5, 0])
    a = np.random.permutation(np.resize(levels, k // 512 * 4)).reshape(k // 512, 4)
    idx = np.arange(k)
    return np.exp2(a[idx // 512, idx % 128 // 32])


BF16 = ml_dtypes.bfloat16


def bf(x):
    return np.asarray(x, np.float32).astype(BF16)


def f64(x):
    return np.asarray(x).astype(np.float64)


B, H, W, C, NS = 2, 2, 1024, 128, 2
WIN = W // NS
SHIFT = WIN // 2


def setup_inputs():
    s = mx_kscale(WIN)
    sv = np.roll(np.tile(s.max() / s, NS), SHIFT)
    return {"q": bf(np.random.standard_normal((B, H * W, C))),
            "k": bf(np.random.standard_normal((B, H * W, C))),
            "v": bf((np.random.standard_normal((B, H, W, C)) * 2.0 * sv[None, None, :, None]).reshape(B, H * W, C)),
            "attn_mask": bf(np.random.standard_normal((NS, WIN, WIN)) + np.log(s)[None, None, :]),
            "h": H, "w": W, "num_splits": NS}


def reference(q, k, v, attn_mask, h, w, num_splits):
    b, hw, c = q.shape
    assert hw == h * w
    win = w // num_splits
    shift = win // 2
    scale = c ** 0.5

    def prep(x):
        x = f64(x).reshape(b * h, w, c)
        x = np.roll(x, -shift, axis=1)
        return x.reshape(b * h, num_splits, win, c)

    qs, ks, vs = prep(q), prep(k), prep(v)
    scores = qs @ ks.transpose(0, 1, 3, 2) / scale
    scores = scores + f64(attn_mask)[None]
    e = np.exp(scores - scores.max(-1, keepdims=True))
    out = (mxq(e, 3, "e4m3") @ mxq(vs, 2, "e4m3")) / e.sum(-1, keepdims=True)
    out = out.reshape(b, h, w, c)
    out = np.roll(out, shift, axis=2)
    return out.reshape(b, h * w, c)

@@ -1,0 +1,183 @@
+from contextlib import ExitStack
+
+import concourse.mybir as mybir
+from concourse.masks import make_identity
+
+BF16 = mybir.dt.bfloat16
+F32 = mybir.dt.float32
+U32 = mybir.dt.uint32
+U8 = mybir.dt.uint8
+FP8X4 = mybir.dt.float8_e4m3fn_x4
+ALU = mybir.AluOpType
+ACT = mybir.ActivationFunctionType
+AX = mybir.AxisListType
+
+P = 128
+C = 128
+ROWS = 4
+WIN = 512
+NWIN = 2
+FLOPS = 2 * (ROWS * NWIN) * 2 * WIN * WIN * C
+
+
+def tile_single_head_split_window_attention_1d_kernel(
+    tc, q, k, v, attn_mask, h, w, num_splits, out
+):
+    nc = tc.nc
+    assert h == 2 and w == 1024 and num_splits == 2
+    scale = 1.0 / (C ** 0.5)
+
+    q_v = q.flatten_outer_dims().rearrange("(g p j) c -> p g j c", p=P, j=2)
+    k_v = k.flatten_outer_dims().rearrange("(t p) c -> p t c", p=P)
+    v_v = v.flatten_outer_dims().rearrange("(t p) c -> p t c", p=P)
+    b_v = attn_mask.rearrange("n (h p j) k -> p n h j k", p=P, j=2)
+    o_v = out.flatten_outer_dims().rearrange("(g p j) c -> p g j c", p=P, j=2)
+
+    with ExitStack() as ctx:
+        const = ctx.enter_context(tc.tile_pool(name="const", bufs=1))
+        work = ctx.enter_context(tc.tile_pool(name="work", bufs=3))
+        ps_t = ctx.enter_context(tc.psum_pool(name="ps_t", bufs=1))
+        ps_s = ctx.enter_context(tc.psum_pool(name="ps_s", bufs=4))
+        ps_e = ctx.enter_context(tc.psum_pool(name="ps_e", bufs=2))
+        ps_o = ctx.enter_context(tc.psum_pool(name="ps_o", bufs=1))
+
+        ident = const.tile([P, P], BF16, name="ident")
+        make_identity(nc, ident[:])
+
+        k_sb = []
+        q_sb = []
+        v_sb = []
+        b_sb = []
+        for r in range(ROWS):
+            k_sb.append(const.tile([P, 8, C], BF16, name="k_sb%d" % r))
+            q_sb.append(const.tile([P, 4, 2, C], BF16, name="q_sb%d" % r))
+            v_sb.append(const.tile([P, 8, C], BF16, name="v_sb%d" % r))
+        for n in range(NWIN):
+            b_sb.append(const.tile([P, 2, 2, WIN], BF16, name="b_sb%d" % n))
+
+        for r in range(ROWS):
+            nc.sync.dma_start(out=k_sb[r][:], in_=k_v[:, 8 * r : 8 * r + 8, :])
+            nc.sync.dma_start(out=q_sb[r][:], in_=q_v[:, 4 * r : 4 * r + 4, :, :])
+            if r == 0:
+                for n in range(NWIN):
+                    nc.sync.dma_start(out=b_sb[n][:], in_=b_v[:, n])
+            nc.sync.dma_start(out=v_sb[r][:], in_=v_v[:, 8 * r : 8 * r + 8, :])
+
+        for r in range(ROWS):
+            gv = work.tile([P, NWIN, C, 4], BF16, name="gv", align_bytes=64)
+            for n in range(NWIN):
+                for hh in range(2):
+                    t0 = (2 + 4 * n + 2 * hh) % 8
+                    nc.vector.tensor_copy(
+                        out=gv[:, n, :, 2 * hh : 2 * hh + 2].rearrange(
+                            "p (c i) t -> p c t i", i=4
+                        ),
+                        in_=v_sb[r][:, t0 : t0 + 2, :].rearrange(
+                            "p t (c i) -> p c t i", i=4
+                        ),
+                    )
+            v_codes = const.tile([P, NWIN * C], U32, name="v_codes%d" % r, align_bytes=64)
+            v_scales = const.tile([P, NWIN * C], U8, name="v_scales%d" % r, align_bytes=64)
+            nc.vector.quantize_mx(
+                out=v_codes[:].bitcast(FP8X4),
+                scales=v_scales[:],
+                in_=gv[:].rearrange("p n c t -> p (n c t)"),
+            )
+
+            for n in range(NWIN):
+                tqk = ps_t.tile([P, 8, P], BF16, name="tqk")
+                for t in range(4):
+                    nc.tensor.transpose(
+                        out=tqk[:, t, :],
+                        in_=k_sb[r][:, (2 + 4 * n + t) % 8, :],
+                        identity=ident[:],
+                    )
+                for a in range(4):
+                    nc.tensor.transpose(
+                        out=tqk[:, 4 + a, :],
+                        in_=q_sb[r][:, (1 + 2 * n + a // 2) % 4, a % 2, :],
+                        identity=ident[:],
+                    )
+                qkT = work.tile([P, 8, P], BF16, name="qkT")
+                nc.vector.tensor_copy(out=qkT[:], in_=tqk[:])
+
+                sp = work.tile([P, 4, WIN], F32, name="sp")
+                for a in range(4):
+                    s_ps = ps_s.tile([P, WIN], F32, name="s_ps")
+                    nc.tensor.matmul(
+                        out=s_ps[:],
+                        lhsT=qkT[:, 4 + a, :],
+                        rhs=qkT[:, 0:4, :].rearrange("p t k -> p (t k)"),
+                        start=True,
+                        stop=True,
+                    )
+                    nc.vector.scalar_tensor_tensor(
+                        out=sp[:, a, :],
+                        in0=s_ps[:],
+                        scalar=scale,
+                        in1=b_sb[n][:, a // 2, a % 2, :],
+                        op0=ALU.mult,
+                        op1=ALU.add,
+                    )
+                negmax = work.tile([P, 4], F32, name="negmax")
+                nc.vector.tensor_reduce(
+                    out=negmax[:], in_=sp[:], axis=AX.X, op=ALU.max, negate=True
+                )
+                e_sb = work.tile([P, 4, WIN], BF16, name="e_sb")
+                rowsum = work.tile([P, 4], F32, name="rowsum")
+                for a in range(4):
+                    nc.scalar.activation(
+                        out=e_sb[:, a, :],
+                        in_=sp[:, a, :],
+                        func=ACT.Exp,
+                        bias=negmax[:, a : a + 1],
+                        scale=1.0,
+                        accum_out=rowsum[:, a : a + 1],
+                    )
+                g_sb = work.tile([P, 4, P, 4], BF16, name="g_sb", align_bytes=64)
+                for b in range(2):
+                    eT = ps_e.tile([P, 2, 4, P], BF16, name="eT")
+                    for a in range(2):
+                        for t in range(4):
+                            nc.tensor.transpose(
+                                out=eT[:, a, t, :],
+                                in_=e_sb[:, 2 * b + a, P * t : P * t + P],
+                                identity=ident[:],
+                            )
+                    nc.scalar.copy(
+                        out=g_sb[:, 2 * b : 2 * b + 2, :, :],
+                        in_=eT[:].rearrange("p a t q -> p a q t"),
+                    )
+                e_codes = work.tile([P, 4 * P], U32, name="e_codes", align_bytes=64)
+                e_scales = work.tile([P, 4 * P], U8, name="e_scales", align_bytes=64)
+                nc.vector.quantize_mx(
+                    out=e_codes[:].bitcast(FP8X4),
+                    scales=e_scales[:],
+                    in_=g_sb[:].rearrange("p a q t -> p (a q t)"),
+                )
+                o_ps = ps_o.tile([P, 4, C], F32, name="o_ps")
+                for a in range(4):
+                    nc.tensor.matmul_mx(
+                        out=o_ps[:, a, :],
+                        lhsT=e_codes[:, P * a : P * a + P].bitcast(FP8X4),
+                        lhsT_scale=e_scales[:, P * a : P * a + P],
+                        rhs=v_codes[:, C * n : C * n + C].bitcast(FP8X4),
+                        rhs_scale=v_scales[:, C * n : C * n + C],
+                        start=True,
+                        stop=True,
+                    )
+                rinv = work.tile([P, 4], F32, name="rinv")
+                nc.vector.reciprocal(out=rinv[:], in_=rowsum[:])
+                o_sb = work.tile([P, 4, C], F32, name="o_sb")
+                for a in range(4):
+                    nc.scalar.activation(
+                        out=o_sb[:, a, :],
+                        in_=o_ps[:, a, :],
+                        func=ACT.Copy,
+                        scale=rinv[:, a : a + 1],
+                    )
+                for hh in range(2):
+                    g = 4 * r + (1 + 2 * n + hh) % 4
+                    nc.sync.dma_start(
+                        out=o_v[:, g, :, :], in_=o_sb[:, 2 * hh : 2 * hh + 2, :]
+                    )

@@ -10,14 +10,15 @@ U8 = mybir.dt.uint8
 FP8X4 = mybir.dt.float8_e4m3fn_x4
 ALU = mybir.AluOpType
 ACT = mybir.ActivationFunctionType
-AX = mybir.AxisListType
 
 P = 128
 C = 128
 ROWS = 4
 WIN = 512
 NWIN = 2
-FLOPS = 2 * (ROWS * NWIN) * 2 * WIN * WIN * C
+UNITS = ROWS * NWIN
+PAIRS = 2 * UNITS
+FLOPS = 2 * UNITS * 2 * WIN * WIN * C
 
 
 def tile_single_head_split_window_attention_1d_kernel(
@@ -35,149 +36,271 @@ def tile_single_head_split_window_attention_1d_kernel(
 
     with ExitStack() as ctx:
         const = ctx.enter_context(tc.tile_pool(name="const", bufs=1))
-        work = ctx.enter_context(tc.tile_pool(name="work", bufs=3))
+        work = ctx.enter_context(tc.tile_pool(name="work", bufs=4))
+        stat = ctx.enter_context(tc.tile_pool(name="stat", bufs=8))
         ps_t = ctx.enter_context(tc.psum_pool(name="ps_t", bufs=1))
         ps_s = ctx.enter_context(tc.psum_pool(name="ps_s", bufs=4))
         ps_e = ctx.enter_context(tc.psum_pool(name="ps_e", bufs=2))
         ps_o = ctx.enter_context(tc.psum_pool(name="ps_o", bufs=1))
+        ctx.enter_context(tc.manual_schedule())
+
+        k_sb = [const.tile([P, 4, C], BF16, name="k_sb%d" % u) for u in range(UNITS)]
+        q_sb = [const.tile([P, 2, 2, C], BF16, name="q_sb%d" % u) for u in range(UNITS)]
+        v_sb = [const.tile([P, 4, C], BF16, name="v_sb%d" % u) for u in range(UNITS)]
+        b_sb = [
+            [const.tile([P, 2, WIN], BF16, name="b_sb%d%d" % (n, hh)) for hh in range(2)]
+            for n in range(NWIN)
+        ]
+
+        def load_tiles(dst, src, u):
+            r, n = u // NWIN, u % NWIN
+            if n == 0:
+                nc.sync.dma_start(out=dst[:], in_=src[:, 8 * r + 2 : 8 * r + 6, :])
+            else:
+                nc.sync.dma_start(out=dst[:, 0:2, :], in_=src[:, 8 * r + 6 : 8 * r + 8, :])
+                nc.sync.dma_start(out=dst[:, 2:4, :], in_=src[:, 8 * r : 8 * r + 2, :])
+
+        def load_q(u):
+            r, n = u // NWIN, u % NWIN
+            if n == 0:
+                nc.sync.dma_start(out=q_sb[u][:], in_=q_v[:, 4 * r + 1 : 4 * r + 3, :, :])
+            else:
+                nc.sync.dma_start(out=q_sb[u][:, 0], in_=q_v[:, 4 * r + 3, :, :])
+                nc.sync.dma_start(out=q_sb[u][:, 1], in_=q_v[:, 4 * r, :, :])
+
+        def load_bias(n):
+            for hh in range(2):
+                nc.sync.dma_start(out=b_sb[n][hh][:], in_=b_v[:, n, hh])
+
+        for u in range(2):
+            load_tiles(k_sb[u], k_v, u)
+            load_q(u)
+            load_bias(u)
+        for u in range(2):
+            load_tiles(v_sb[u], v_v, u)
+        for u in range(2, UNITS):
+            load_tiles(k_sb[u], k_v, u)
+            load_q(u)
+            load_tiles(v_sb[u], v_v, u)
 
         ident = const.tile([P, P], BF16, name="ident")
         make_identity(nc, ident[:])
+        ident_f = const.tile([P, P], F32, name="ident_f")
+        make_identity(nc, ident_f[:])
+        warm = const.tile([P, 1], F32, name="warm")
+        nc.vector.memset(warm[:], 0.0)
+        warm2 = const.tile([P, 1], F32, name="warm2")
+        nc.scalar.activation(out=warm2[:], in_=warm[:], func=ACT.Exp)
 
-        k_sb = []
-        q_sb = []
-        v_sb = []
-        b_sb = []
-        for r in range(ROWS):
-            k_sb.append(const.tile([P, 8, C], BF16, name="k_sb%d" % r))
-            q_sb.append(const.tile([P, 4, 2, C], BF16, name="q_sb%d" % r))
-            v_sb.append(const.tile([P, 8, C], BF16, name="v_sb%d" % r))
-        for n in range(NWIN):
-            b_sb.append(const.tile([P, 2, 2, WIN], BF16, name="b_sb%d" % n))
+        bp = [const.tile([P, 4, 4, P], F32, name="bp%d" % n) for n in range(NWIN)]
+        v_codes = [const.tile([P, C], U32, name="v_codes%d" % u, align_bytes=64) for u in range(UNITS)]
+        v_scales = [const.tile([P, C], U8, name="v_scales%d" % u, align_bytes=64) for u in range(UNITS)]
 
-        for r in range(ROWS):
-            nc.sync.dma_start(out=k_sb[r][:], in_=k_v[:, 8 * r : 8 * r + 8, :])
-            nc.sync.dma_start(out=q_sb[r][:], in_=q_v[:, 4 * r : 4 * r + 4, :, :])
-            if r == 0:
-                for n in range(NWIN):
-                    nc.sync.dma_start(out=b_sb[n][:], in_=b_v[:, n])
-            nc.sync.dma_start(out=v_sb[r][:], in_=v_v[:, 8 * r : 8 * r + 8, :])
+        live = {}
 
-        for r in range(ROWS):
-            gv = work.tile([P, NWIN, C, 4], BF16, name="gv", align_bytes=64)
-            for n in range(NWIN):
-                for hh in range(2):
-                    t0 = (2 + 4 * n + 2 * hh) % 8
-                    nc.vector.tensor_copy(
-                        out=gv[:, n, :, 2 * hh : 2 * hh + 2].rearrange(
-                            "p (c i) t -> p c t i", i=4
-                        ),
-                        in_=v_sb[r][:, t0 : t0 + 2, :].rearrange(
-                            "p t (c i) -> p c t i", i=4
-                        ),
-                    )
-            v_codes = const.tile([P, NWIN * C], U32, name="v_codes%d" % r, align_bytes=64)
-            v_scales = const.tile([P, NWIN * C], U8, name="v_scales%d" % r, align_bytes=64)
-            nc.vector.quantize_mx(
-                out=v_codes[:].bitcast(FP8X4),
-                scales=v_scales[:],
-                in_=gv[:].rearrange("p n c t -> p (n c t)"),
-            )
-
-            for n in range(NWIN):
-                tqk = ps_t.tile([P, 8, P], BF16, name="tqk")
+        def bias_t(n, a0, na):
+            bT = ps_e.tile([P, na, 4, P], BF16, name="bT", tag="eT")
+            for a in range(na):
                 for t in range(4):
                     nc.tensor.transpose(
-                        out=tqk[:, t, :],
-                        in_=k_sb[r][:, (2 + 4 * n + t) % 8, :],
+                        out=bT[:, a, t, :],
+                        in_=b_sb[n][(a0 + a) // 2][:, (a0 + a) % 2, P * t : P * t + P],
                         identity=ident[:],
                     )
-                for a in range(4):
-                    nc.tensor.transpose(
-                        out=tqk[:, 4 + a, :],
-                        in_=q_sb[r][:, (1 + 2 * n + a // 2) % 4, a % 2, :],
-                        identity=ident[:],
-                    )
-                qkT = work.tile([P, 8, P], BF16, name="qkT")
-                nc.vector.tensor_copy(out=qkT[:], in_=tqk[:])
+            live["bT", n, a0] = bT
 
-                sp = work.tile([P, 4, WIN], F32, name="sp")
-                for a in range(4):
-                    s_ps = ps_s.tile([P, WIN], F32, name="s_ps")
-                    nc.tensor.matmul(
-                        out=s_ps[:],
-                        lhsT=qkT[:, 4 + a, :],
-                        rhs=qkT[:, 0:4, :].rearrange("p t k -> p (t k)"),
-                        start=True,
-                        stop=True,
-                    )
-                    nc.vector.scalar_tensor_tensor(
-                        out=sp[:, a, :],
-                        in0=s_ps[:],
-                        scalar=scale,
-                        in1=b_sb[n][:, a // 2, a % 2, :],
-                        op0=ALU.mult,
-                        op1=ALU.add,
-                    )
-                negmax = work.tile([P, 4], F32, name="negmax")
-                nc.vector.tensor_reduce(
-                    out=negmax[:], in_=sp[:], axis=AX.X, op=ALU.max, negate=True
+        def bias_ev(n, a0, na, on_vector):
+            bT = live["bT", n, a0]
+            if on_vector:
+                nc.vector.tensor_scalar_mul(
+                    out=bp[n][:, a0 : a0 + na, :, :], in0=bT[:], scalar1=C ** 0.5
                 )
-                e_sb = work.tile([P, 4, WIN], BF16, name="e_sb")
-                rowsum = work.tile([P, 4], F32, name="rowsum")
-                for a in range(4):
-                    nc.scalar.activation(
-                        out=e_sb[:, a, :],
-                        in_=sp[:, a, :],
-                        func=ACT.Exp,
-                        bias=negmax[:, a : a + 1],
-                        scale=1.0,
-                        accum_out=rowsum[:, a : a + 1],
-                    )
-                g_sb = work.tile([P, 4, P, 4], BF16, name="g_sb", align_bytes=64)
-                for b in range(2):
-                    eT = ps_e.tile([P, 2, 4, P], BF16, name="eT")
-                    for a in range(2):
-                        for t in range(4):
-                            nc.tensor.transpose(
-                                out=eT[:, a, t, :],
-                                in_=e_sb[:, 2 * b + a, P * t : P * t + P],
-                                identity=ident[:],
-                            )
-                    nc.scalar.copy(
-                        out=g_sb[:, 2 * b : 2 * b + 2, :, :],
-                        in_=eT[:].rearrange("p a t q -> p a q t"),
-                    )
-                e_codes = work.tile([P, 4 * P], U32, name="e_codes", align_bytes=64)
-                e_scales = work.tile([P, 4 * P], U8, name="e_scales", align_bytes=64)
-                nc.vector.quantize_mx(
-                    out=e_codes[:].bitcast(FP8X4),
-                    scales=e_scales[:],
-                    in_=g_sb[:].rearrange("p a q t -> p (a q t)"),
+            else:
+                nc.scalar.mul(out=bp[n][:, a0 : a0 + na, :, :], in_=bT[:], mul=C ** 0.5)
+
+        def tqk(u):
+            t_ps = ps_t.tile([P, 8, P], BF16, name="t_ps")
+            for t in range(4):
+                nc.tensor.transpose(out=t_ps[:, t, :], in_=k_sb[u][:, t, :], identity=ident[:])
+            for a in range(4):
+                nc.tensor.transpose(
+                    out=t_ps[:, 4 + a, :], in_=q_sb[u][:, a // 2, a % 2, :], identity=ident[:]
                 )
-                o_ps = ps_o.tile([P, 4, C], F32, name="o_ps")
-                for a in range(4):
-                    nc.tensor.matmul_mx(
-                        out=o_ps[:, a, :],
-                        lhsT=e_codes[:, P * a : P * a + P].bitcast(FP8X4),
-                        lhsT_scale=e_scales[:, P * a : P * a + P],
-                        rhs=v_codes[:, C * n : C * n + C].bitcast(FP8X4),
-                        rhs_scale=v_scales[:, C * n : C * n + C],
-                        start=True,
-                        stop=True,
+            live["t_ps", u] = t_ps
+
+        def evqk(u):
+            qkT = work.tile([P, 8, P], BF16, name="qkT")
+            nc.vector.tensor_copy(out=qkT[:], in_=live["t_ps", u][:])
+            live["qkT", u] = qkT
+
+        def vprep(u):
+            gv = work.tile([P, C, 4], BF16, name="gv", align_bytes=64)
+            nc.vector.tensor_copy(
+                out=gv[:].rearrange("p (c i) t -> p c t i", i=4),
+                in_=v_sb[u][:].rearrange("p t (c i) -> p c t i", i=4),
+            )
+            live["gv", u] = gv
+
+        def vquant(u):
+            nc.vector.quantize_mx(
+                out=v_codes[u][:].bitcast(FP8X4),
+                scales=v_scales[u][:],
+                in_=live["gv", u][:].rearrange("p c t -> p (c t)"),
+            )
+
+        def score(i):
+            u, a = i // 4, i % 4
+            qkT = live["qkT", u]
+            s_ps = ps_s.tile([P, WIN], F32, name="s_ps")
+            nc.tensor.matmul(
+                out=s_ps[:],
+                lhsT=qkT[:, 4 + a, :],
+                rhs=qkT[:, 0:4, :].rearrange("p t k -> p (t k)"),
+                start=True,
+                stop=False,
+            )
+            for t in range(4):
+                nc.tensor.matmul(
+                    out=s_ps[:, P * t : P * t + P],
+                    lhsT=bp[u % NWIN][:, a, t, :],
+                    rhs=ident_f[:],
+                    is_transpose=True,
+                    start=False,
+                    stop=(t == 3),
+                )
+            live["s_ps", i] = s_ps
+
+        def rowmax(i):
+            sp = work.tile([P, WIN], F32, name="sp")
+            negmax = stat.tile([P, 1], F32, name="negmax")
+            nc.vector.tensor_scalar(
+                out=sp[:],
+                in0=live["s_ps", i][:],
+                scalar1=-scale,
+                scalar2=None,
+                op0=ALU.mult,
+                op1=ALU.min,
+                accum_out=negmax[:],
+            )
+            live["sp", i] = (sp, negmax)
+
+        def expo(i):
+            j, a = i // 2, i % 2
+            if a == 0:
+                live["e", j] = (
+                    work.tile([P, 2, WIN], BF16, name="e_sb"),
+                    stat.tile([P, 2], F32, name="rowsum"),
+                )
+            e_sb, rowsum = live["e", j]
+            sp, negmax = live["sp", i]
+            nc.scalar.activation(
+                out=e_sb[:, a, :],
+                in_=sp[:],
+                func=ACT.Exp,
+                bias=negmax[:],
+                scale=-1.0,
+                accum_out=rowsum[:, a : a + 1],
+            )
+
+        def te(j):
+            e_sb = live["e", j][0]
+            eT = ps_e.tile([P, 2, 4, P], BF16, name="eT")
+            for a in range(2):
+                for t in range(4):
+                    nc.tensor.transpose(
+                        out=eT[:, a, t, :], in_=e_sb[:, a, P * t : P * t + P], identity=ident[:]
                     )
-                rinv = work.tile([P, 4], F32, name="rinv")
-                nc.vector.reciprocal(out=rinv[:], in_=rowsum[:])
-                o_sb = work.tile([P, 4, C], F32, name="o_sb")
-                for a in range(4):
-                    nc.scalar.activation(
-                        out=o_sb[:, a, :],
-                        in_=o_ps[:, a, :],
-                        func=ACT.Copy,
-                        scale=rinv[:, a : a + 1],
-                    )
-                for hh in range(2):
-                    g = 4 * r + (1 + 2 * n + hh) % 4
-                    nc.sync.dma_start(
-                        out=o_v[:, g, :, :], in_=o_sb[:, 2 * hh : 2 * hh + 2, :]
-                    )
+            live["eT", j] = eT
+
+        def eve(j):
+            g_sb = work.tile([P, 2, P, 4], BF16, name="g_sb", align_bytes=64)
+            src = live["eT", j][:].rearrange("p a t q -> p a q t")
+            nc.scalar.copy(out=g_sb[:], in_=src)
+            live["g", j] = g_sb
+
+        def qnt(j):
+            e_codes = work.tile([P, 2 * P], U32, name="e_codes", align_bytes=64)
+            e_scales = work.tile([P, 2 * P], U8, name="e_scales", align_bytes=64)
+            nc.vector.quantize_mx(
+                out=e_codes[:].bitcast(FP8X4),
+                scales=e_scales[:],
+                in_=live["g", j][:].rearrange("p a q t -> p (a q t)"),
+            )
+            live["c", j] = (e_codes, e_scales)
+
+        def mxp(j):
+            u = j // 2
+            e_codes, e_scales = live["c", j]
+            o_ps = ps_o.tile([P, 2, C], F32, name="o_ps")
+            for a in range(2):
+                nc.tensor.matmul_mx(
+                    out=o_ps[:, a, :],
+                    lhsT=e_codes[:, P * a : P * a + P].bitcast(FP8X4),
+                    lhsT_scale=e_scales[:, P * a : P * a + P],
+                    rhs=v_codes[u][:].bitcast(FP8X4),
+                    rhs_scale=v_scales[u][:],
+                    start=True,
+                    stop=True,
+                )
+            live["o", j] = o_ps
+
+        def outp(j):
+            u, hh = j // 2, j % 2
+            r, n = u // NWIN, u % NWIN
+            rowsum = live["e", j][1]
+            o_ps = live["o", j]
+            rinv = stat.tile([P, 2], F32, name="rinv")
+            nc.vector.reciprocal(out=rinv[:], in_=rowsum[:])
+            o_sb = work.tile([P, 2, C], F32, name="o_sb")
+            nc.vector.tensor_tensor(
+                out=o_sb[:],
+                in0=o_ps[:],
+                in1=rinv[:].unsqueeze(2).to_broadcast([P, 2, C]),
+                op=ALU.mult,
+            )
+            g = 4 * r + (1 + 2 * n + hh) % 4
+            nc.sync.dma_start(out=o_v[:, g, :, :], in_=o_sb[:])
+
+        def bias_prep(n, na):
+            for a0 in range(0, 4, 2 * na):
+                bias_t(n, a0, na)
+                bias_t(n, a0 + na, na)
+                bias_ev(n, a0, na, True)
+                bias_ev(n, a0 + na, na, False)
+
+        tqk(0)
+        evqk(0)
+        bias_prep(0, 1)
+
+        LAG_MX = 5
+        for s in range(PAIRS + LAG_MX + 1):
+            if s < PAIRS:
+                score(2 * s)
+                score(2 * s + 1)
+            if 0 <= s - LAG_MX < PAIRS:
+                mxp(s - LAG_MX)
+            if s % 2 == 0 and s // 2 + 1 < UNITS:
+                tqk(s // 2 + 1)
+            if 0 <= s - 2 < PAIRS:
+                te(s - 2)
+            m = s - 1
+            if 0 <= m < PAIRS:
+                rowmax(2 * m)
+                rowmax(2 * m + 1)
+            if m >= 0 and m % 2 == 0 and m // 2 + 1 < UNITS:
+                evqk(m // 2 + 1)
+            if m >= 0 and m % 2 == 0 and m // 2 < UNITS:
+                vprep(m // 2)
+            if 0 <= m - 3 < PAIRS:
+                qnt(m - 3)
+            if m >= 0 and m % 2 == 0 and m // 2 < UNITS:
+                vquant(m // 2)
+            if 0 <= m - (LAG_MX - 1) < PAIRS:
+                outp(m - (LAG_MX - 1))
+            if 0 <= m < PAIRS:
+                expo(2 * m)
+                expo(2 * m + 1)
+            if 0 <= m - 1 < PAIRS:
+                eve(m - 1)
+            if s == 1:
+                bias_prep(1, 2)

@@ -10,6 +10,7 @@ U8 = mybir.dt.uint8
 FP8X4 = mybir.dt.float8_e4m3fn_x4
 ALU = mybir.AluOpType
 ACT = mybir.ActivationFunctionType
+AX = mybir.AxisListType
 
 P = 128
 C = 128
@@ -19,6 +20,8 @@ NWIN = 2
 UNITS = ROWS * NWIN
 PAIRS = 2 * UNITS
 FLOPS = 2 * UNITS * 2 * WIN * WIN * C
+VPATH = (3,)
+DIRECT = (14, 15)
 
 
 def tile_single_head_split_window_attention_1d_kernel(
@@ -53,7 +56,7 @@ def tile_single_head_split_window_attention_1d_kernel(
         ]
 
         def load_tiles(dst, src, u):
-            r, n = u // NWIN, u % NWIN
+            r, n = u % ROWS, u // ROWS
             if n == 0:
                 nc.sync.dma_start(out=dst[:], in_=src[:, 8 * r + 2 : 8 * r + 6, :])
             else:
@@ -61,7 +64,7 @@ def tile_single_head_split_window_attention_1d_kernel(
                 nc.sync.dma_start(out=dst[:, 2:4, :], in_=src[:, 8 * r : 8 * r + 2, :])
 
         def load_q(u):
-            r, n = u // NWIN, u % NWIN
+            r, n = u % ROWS, u // ROWS
             if n == 0:
                 nc.sync.dma_start(out=q_sb[u][:], in_=q_v[:, 4 * r + 1 : 4 * r + 3, :, :])
             else:
@@ -72,16 +75,16 @@ def tile_single_head_split_window_attention_1d_kernel(
             for hh in range(2):
                 nc.sync.dma_start(out=b_sb[n][hh][:], in_=b_v[:, n, hh])
 
-        for u in range(2):
+        for u in range(UNITS):
             load_tiles(k_sb[u], k_v, u)
             load_q(u)
-            load_bias(u)
-        for u in range(2):
-            load_tiles(v_sb[u], v_v, u)
-        for u in range(2, UNITS):
-            load_tiles(k_sb[u], k_v, u)
-            load_q(u)
-            load_tiles(v_sb[u], v_v, u)
+            if u == 0:
+                load_bias(0)
+            else:
+                load_tiles(v_sb[u - 1], v_v, u - 1)
+            if u == 2:
+                load_bias(1)
+        load_tiles(v_sb[UNITS - 1], v_v, UNITS - 1)
 
         ident = const.tile([P, P], BF16, name="ident")
         make_identity(nc, ident[:])
@@ -98,8 +101,11 @@ def tile_single_head_split_window_attention_1d_kernel(
 
         live = {}
 
-        def bias_t(n, a0, na):
-            bT = ps_e.tile([P, na, 4, P], BF16, name="bT", tag="eT")
+        def bias_t(n, a0, na, spare):
+            if spare:
+                bT = ps_o.tile([P, na, 4, P], BF16, name="bT", tag="o_ps")
+            else:
+                bT = ps_e.tile([P, na, 4, P], BF16, name="bT", tag="eT")
             for a in range(na):
                 for t in range(4):
                     nc.tensor.transpose(
@@ -128,16 +134,23 @@ def tile_single_head_split_window_attention_1d_kernel(
                 )
             live["t_ps", u] = t_ps
 
-        def evqk(u):
+        def evqk(u, on_vector):
             qkT = work.tile([P, 8, P], BF16, name="qkT")
-            nc.vector.tensor_copy(out=qkT[:], in_=live["t_ps", u][:])
+            if on_vector:
+                nc.vector.tensor_copy(out=qkT[:], in_=live["t_ps", u][:])
+            else:
+                nc.scalar.copy(out=qkT[:], in_=live["t_ps", u][:])
             live["qkT", u] = qkT
 
         def vprep(u):
             gv = work.tile([P, C, 4], BF16, name="gv", align_bytes=64)
-            nc.vector.tensor_copy(
-                out=gv[:].rearrange("p (c i) t -> p c t i", i=4),
-                in_=v_sb[u][:].rearrange("p t (c i) -> p c t i", i=4),
+            nc.gpsimd.tensor_scalar(
+                out=gv[:],
+                in0=v_sb[u][:].rearrange("p t c -> p c t"),
+                scalar1=1.0,
+                scalar2=0.0,
+                op0=ALU.mult,
+                op1=ALU.add,
             )
             live["gv", u] = gv
 
@@ -157,82 +170,120 @@ def tile_single_head_split_window_attention_1d_kernel(
                 lhsT=qkT[:, 4 + a, :],
                 rhs=qkT[:, 0:4, :].rearrange("p t k -> p (t k)"),
                 start=True,
-                stop=False,
+                stop=(a in VPATH),
             )
-            for t in range(4):
-                nc.tensor.matmul(
-                    out=s_ps[:, P * t : P * t + P],
-                    lhsT=bp[u % NWIN][:, a, t, :],
-                    rhs=ident_f[:],
-                    is_transpose=True,
-                    start=False,
-                    stop=(t == 3),
-                )
+            if a not in VPATH:
+                for t in range(4):
+                    nc.tensor.matmul(
+                        out=s_ps[:, P * t : P * t + P],
+                        lhsT=bp[u // ROWS][:, a, t, :],
+                        rhs=ident_f[:],
+                        is_transpose=True,
+                        start=False,
+                        stop=(t == 3),
+                    )
             live["s_ps", i] = s_ps
 
         def rowmax(i):
+            u, a = i // 4, i % 4
             sp = work.tile([P, WIN], F32, name="sp")
             negmax = stat.tile([P, 1], F32, name="negmax")
-            nc.vector.tensor_scalar(
-                out=sp[:],
-                in0=live["s_ps", i][:],
-                scalar1=-scale,
-                scalar2=None,
-                op0=ALU.mult,
-                op1=ALU.min,
-                accum_out=negmax[:],
-            )
+            if a in VPATH:
+                nc.vector.scalar_tensor_tensor(
+                    out=sp[:],
+                    in0=live["s_ps", i][:],
+                    scalar=scale,
+                    in1=b_sb[u // ROWS][a // 2][:, a % 2, :],
+                    op0=ALU.mult,
+                    op1=ALU.add,
+                )
+                nc.vector.tensor_reduce(
+                    out=negmax[:], in_=sp[:], axis=AX.X, op=ALU.max, negate=True
+                )
+            else:
+                nc.vector.tensor_scalar(
+                    out=sp[:],
+                    in0=live["s_ps", i][:],
+                    scalar1=-scale,
+                    scalar2=None,
+                    op0=ALU.mult,
+                    op1=ALU.min,
+                    accum_out=negmax[:],
+                )
             live["sp", i] = (sp, negmax)
 
         def expo(i):
-            j, a = i // 2, i % 2
+            u, a = i // 4, i % 4
             if a == 0:
-                live["e", j] = (
-                    work.tile([P, 2, WIN], BF16, name="e_sb"),
-                    stat.tile([P, 2], F32, name="rowsum"),
-                )
-            e_sb, rowsum = live["e", j]
+                live["rowsum", u] = stat.tile([P, 4], F32, name="rowsum")
+            if a % 2 == 0:
+                live["e", i // 2] = work.tile([P, 2, WIN], BF16, name="e_sb")
             sp, negmax = live["sp", i]
             nc.scalar.activation(
-                out=e_sb[:, a, :],
+                out=live["e", i // 2][:, a % 2, :],
                 in_=sp[:],
                 func=ACT.Exp,
                 bias=negmax[:],
-                scale=-1.0,
-                accum_out=rowsum[:, a : a + 1],
+                scale=(1.0 if a in VPATH else -1.0),
+                accum_out=live["rowsum", u][:, a : a + 1],
             )
 
-        def te(j):
-            e_sb = live["e", j][0]
-            eT = ps_e.tile([P, 2, 4, P], BF16, name="eT")
-            for a in range(2):
-                for t in range(4):
-                    nc.tensor.transpose(
-                        out=eT[:, a, t, :], in_=e_sb[:, a, P * t : P * t + P], identity=ident[:]
-                    )
-            live["eT", j] = eT
+        def teh(i):
+            j, a = i // 2, i % 2
+            if a == 0:
+                live["eT", j] = ps_e.tile([P, 2, 4, P], BF16, name="eT")
+            for t in range(4):
+                nc.tensor.transpose(
+                    out=live["eT", j][:, a, t, :],
+                    in_=live["e", j][:, a, P * t : P * t + P],
+                    identity=ident[:],
+                )
 
         def eve(j):
-            g_sb = work.tile([P, 2, P, 4], BF16, name="g_sb", align_bytes=64)
-            src = live["eT", j][:].rearrange("p a t q -> p a q t")
-            nc.scalar.copy(out=g_sb[:], in_=src)
-            live["g", j] = g_sb
+            eT = live["eT", j]
+            if j in DIRECT:
+                g_sb = work.tile([P, 2, P, 4], BF16, name="g_sb", align_bytes=64)
+                if j % 2 == 0:
+                    nc.scalar.copy(out=g_sb[:], in_=eT[:].rearrange("p a t q -> p a q t"))
+                else:
+                    nc.vector.tensor_copy(out=g_sb[:], in_=eT[:].rearrange("p a t q -> p a q t"))
+                live["g", j] = g_sb
+            else:
+                x_sb = work.tile([P, 2, 4, P], BF16, name="x_sb")
+                nc.scalar.copy(out=x_sb[:], in_=eT[:])
+                live["x", j] = x_sb
+
+        def gi(j):
+            if j not in DIRECT:
+                g_sb = work.tile([P, 2, P, 4], BF16, name="g_sb", align_bytes=64)
+                nc.gpsimd.tensor_scalar(
+                    out=g_sb[:],
+                    in0=live["x", j][:].rearrange("p a t q -> p a q t"),
+                    scalar1=1.0,
+                    scalar2=0.0,
+                    op0=ALU.mult,
+                    op1=ALU.add,
+                )
+                live["g", j] = g_sb
 
         def qnt(j):
-            e_codes = work.tile([P, 2 * P], U32, name="e_codes", align_bytes=64)
-            e_scales = work.tile([P, 2 * P], U8, name="e_scales", align_bytes=64)
+            u, b = j // 2, j % 2
+            if b == 0:
+                live["c", u] = (
+                    work.tile([P, 4 * P], U32, name="e_codes", align_bytes=64),
+                    work.tile([P, 4 * P], U8, name="e_scales", align_bytes=64),
+                )
+            e_codes, e_scales = live["c", u]
             nc.vector.quantize_mx(
-                out=e_codes[:].bitcast(FP8X4),
-                scales=e_scales[:],
+                out=e_codes[:, 2 * P * b : 2 * P * b + 2 * P].bitcast(FP8X4),
+                scales=e_scales[:, 2 * P * b : 2 * P * b + 2 * P],
                 in_=live["g", j][:].rearrange("p a q t -> p (a q t)"),
             )
-            live["c", j] = (e_codes, e_scales)
 
-        def mxp(j):
-            u = j // 2
-            e_codes, e_scales = live["c", j]
-            o_ps = ps_o.tile([P, 2, C], F32, name="o_ps")
-            for a in range(2):
+        def mxu(u):
+            e_codes, e_scales = live["c", u]
+            o_ps = ps_o.tile([P, 4, C], F32, name="o_ps")
+            for a in range(4):
                 nc.tensor.matmul_mx(
                     out=o_ps[:, a, :],
                     lhsT=e_codes[:, P * a : P * a + P].bitcast(FP8X4),
@@ -242,65 +293,65 @@ def tile_single_head_split_window_attention_1d_kernel(
                     start=True,
                     stop=True,
                 )
-            live["o", j] = o_ps
+            live["o", u] = o_ps
 
-        def outp(j):
-            u, hh = j // 2, j % 2
-            r, n = u // NWIN, u % NWIN
-            rowsum = live["e", j][1]
-            o_ps = live["o", j]
-            rinv = stat.tile([P, 2], F32, name="rinv")
-            nc.vector.reciprocal(out=rinv[:], in_=rowsum[:])
-            o_sb = work.tile([P, 2, C], F32, name="o_sb")
+        def outu(u):
+            r, n = u % ROWS, u // ROWS
+            rinv = stat.tile([P, 4], F32, name="rinv")
+            nc.vector.reciprocal(out=rinv[:], in_=live["rowsum", u][:])
+            o_sb = work.tile([P, 4, C], F32, name="o_sb")
             nc.vector.tensor_tensor(
                 out=o_sb[:],
-                in0=o_ps[:],
-                in1=rinv[:].unsqueeze(2).to_broadcast([P, 2, C]),
+                in0=live["o", u][:],
+                in1=rinv[:].unsqueeze(2).to_broadcast([P, 4, C]),
                 op=ALU.mult,
             )
-            g = 4 * r + (1 + 2 * n + hh) % 4
-            nc.sync.dma_start(out=o_v[:, g, :, :], in_=o_sb[:])
-
-        def bias_prep(n, na):
-            for a0 in range(0, 4, 2 * na):
-                bias_t(n, a0, na)
-                bias_t(n, a0 + na, na)
-                bias_ev(n, a0, na, True)
-                bias_ev(n, a0 + na, na, False)
+            for hh in range(2):
+                g = 4 * r + (1 + 2 * n + hh) % 4
+                nc.sync.dma_start(out=o_v[:, g, :, :], in_=o_sb[:, 2 * hh : 2 * hh + 2, :])
 
         tqk(0)
-        evqk(0)
-        bias_prep(0, 1)
+        evqk(0, True)
+        bias_t(0, 0, 1, False)
+        bias_t(0, 1, 1, False)
+        bias_t(0, 2, 1, True)
+        bias_ev(0, 0, 1, True)
+        bias_ev(0, 1, 1, False)
+        bias_ev(0, 2, 1, True)
 
-        LAG_MX = 5
-        for s in range(PAIRS + LAG_MX + 1):
-            if s < PAIRS:
-                score(2 * s)
-                score(2 * s + 1)
-            if 0 <= s - LAG_MX < PAIRS:
-                mxp(s - LAG_MX)
+        for s in range(PAIRS + 7):
+            for a in range(2):
+                if s < PAIRS:
+                    score(2 * s + a)
+                if 0 <= s - 2 < PAIRS:
+                    teh(2 * (s - 2) + a)
+            if s % 2 == 0 and 0 <= (s - 6) // 2 < UNITS:
+                mxu((s - 6) // 2)
             if s % 2 == 0 and s // 2 + 1 < UNITS:
                 tqk(s // 2 + 1)
+            if 0 <= s - 1 < PAIRS:
+                rowmax(2 * (s - 1))
+                rowmax(2 * (s - 1) + 1)
+            if 0 <= s - 4 < PAIRS:
+                qnt(s - 4)
+            if s % 2 == 0 and 0 <= (s - 2) // 2 < UNITS:
+                vquant((s - 2) // 2)
+            if s % 2 == 0 and 0 <= (s - 6) // 2 < UNITS:
+                outu((s - 6) // 2)
+            if 0 <= s - 1 < PAIRS:
+                expo(2 * (s - 1))
+                expo(2 * (s - 1) + 1)
             if 0 <= s - 2 < PAIRS:
-                te(s - 2)
-            m = s - 1
-            if 0 <= m < PAIRS:
-                rowmax(2 * m)
-                rowmax(2 * m + 1)
-            if m >= 0 and m % 2 == 0 and m // 2 + 1 < UNITS:
-                evqk(m // 2 + 1)
-            if m >= 0 and m % 2 == 0 and m // 2 < UNITS:
-                vprep(m // 2)
-            if 0 <= m - 3 < PAIRS:
-                qnt(m - 3)
-            if m >= 0 and m % 2 == 0 and m // 2 < UNITS:
-                vquant(m // 2)
-            if 0 <= m - (LAG_MX - 1) < PAIRS:
-                outp(m - (LAG_MX - 1))
-            if 0 <= m < PAIRS:
-                expo(2 * m)
-                expo(2 * m + 1)
-            if 0 <= m - 1 < PAIRS:
-                eve(m - 1)
-            if s == 1:
-                bias_prep(1, 2)
+                eve(s - 2)
+            if s % 2 == 0 and s // 2 + 1 < UNITS:
+                evqk(s // 2 + 1, False)
+            if 0 <= s - 2 < PAIRS:
+                gi(s - 2)
+            if s % 2 == 1 and s // 2 < UNITS:
+                vprep(s // 2)
+            if s == 2:
+                bias_t(1, 0, 2, True)
+                bias_ev(1, 0, 2, True)
+            if s == 4:
+                bias_t(1, 2, 1, True)
+                bias_ev(1, 2, 1, True)

@@ -7,10 +7,10 @@ BF16 = mybir.dt.bfloat16
 F32 = mybir.dt.float32
 U32 = mybir.dt.uint32
 U8 = mybir.dt.uint8
+I32 = mybir.dt.int32
 FP8X4 = mybir.dt.float8_e4m3fn_x4
 ALU = mybir.AluOpType
 ACT = mybir.ActivationFunctionType
-AX = mybir.AxisListType
 
 P = 128
 C = 128
@@ -20,8 +20,6 @@ NWIN = 2
 UNITS = ROWS * NWIN
 PAIRS = 2 * UNITS
 FLOPS = 2 * UNITS * 2 * WIN * WIN * C
-VPATH = (3,)
-DIRECT = (14, 15)
 
 
 def tile_single_head_split_window_attention_1d_kernel(
@@ -82,7 +80,7 @@ def tile_single_head_split_window_attention_1d_kernel(
                 load_bias(0)
             else:
                 load_tiles(v_sb[u - 1], v_v, u - 1)
-            if u == 2:
+            if u == 1:
                 load_bias(1)
         load_tiles(v_sb[UNITS - 1], v_v, UNITS - 1)
 
@@ -134,23 +132,16 @@ def tile_single_head_split_window_attention_1d_kernel(
                 )
             live["t_ps", u] = t_ps
 
-        def evqk(u, on_vector):
+        def evqk(u):
             qkT = work.tile([P, 8, P], BF16, name="qkT")
-            if on_vector:
-                nc.vector.tensor_copy(out=qkT[:], in_=live["t_ps", u][:])
-            else:
-                nc.scalar.copy(out=qkT[:], in_=live["t_ps", u][:])
+            nc.vector.tensor_copy(out=qkT[:], in_=live["t_ps", u][:])
             live["qkT", u] = qkT
 
         def vprep(u):
             gv = work.tile([P, C, 4], BF16, name="gv", align_bytes=64)
-            nc.gpsimd.tensor_scalar(
-                out=gv[:],
-                in0=v_sb[u][:].rearrange("p t c -> p c t"),
-                scalar1=1.0,
-                scalar2=0.0,
-                op0=ALU.mult,
-                op1=ALU.add,
+            nc.vector.tensor_copy(
+                out=gv[:].rearrange("p (c i) t -> p c t i", i=4),
+                in_=v_sb[u][:].rearrange("p t (c i) -> p c t i", i=4),
             )
             live["gv", u] = gv
 
@@ -161,7 +152,7 @@ def tile_single_head_split_window_attention_1d_kernel(
                 in_=live["gv", u][:].rearrange("p c t -> p (c t)"),
             )
 
-        def score(i):
+        def qk(i):
             u, a = i // 4, i % 4
             qkT = live["qkT", u]
             s_ps = ps_s.tile([P, WIN], F32, name="s_ps")
@@ -170,46 +161,34 @@ def tile_single_head_split_window_attention_1d_kernel(
                 lhsT=qkT[:, 4 + a, :],
                 rhs=qkT[:, 0:4, :].rearrange("p t k -> p (t k)"),
                 start=True,
-                stop=(a in VPATH),
+                stop=False,
             )
-            if a not in VPATH:
-                for t in range(4):
-                    nc.tensor.matmul(
-                        out=s_ps[:, P * t : P * t + P],
-                        lhsT=bp[u // ROWS][:, a, t, :],
-                        rhs=ident_f[:],
-                        is_transpose=True,
-                        start=False,
-                        stop=(t == 3),
-                    )
             live["s_ps", i] = s_ps
 
-        def rowmax(i):
+        def addbias(i):
             u, a = i // 4, i % 4
+            for t in range(4):
+                nc.tensor.matmul(
+                    out=live["s_ps", i][:, P * t : P * t + P],
+                    lhsT=bp[u // ROWS][:, a, t, :],
+                    rhs=ident_f[:],
+                    is_transpose=True,
+                    start=False,
+                    stop=(t == 3),
+                )
+
+        def rowmax(i):
             sp = work.tile([P, WIN], F32, name="sp")
             negmax = stat.tile([P, 1], F32, name="negmax")
-            if a in VPATH:
-                nc.vector.scalar_tensor_tensor(
-                    out=sp[:],
-                    in0=live["s_ps", i][:],
-                    scalar=scale,
-                    in1=b_sb[u // ROWS][a // 2][:, a % 2, :],
-                    op0=ALU.mult,
-                    op1=ALU.add,
-                )
-                nc.vector.tensor_reduce(
-                    out=negmax[:], in_=sp[:], axis=AX.X, op=ALU.max, negate=True
-                )
-            else:
-                nc.vector.tensor_scalar(
-                    out=sp[:],
-                    in0=live["s_ps", i][:],
-                    scalar1=-scale,
-                    scalar2=None,
-                    op0=ALU.mult,
-                    op1=ALU.min,
-                    accum_out=negmax[:],
-                )
+            nc.vector.tensor_scalar(
+                out=sp[:],
+                in0=live["s_ps", i][:],
+                scalar1=-scale,
+                scalar2=None,
+                op0=ALU.mult,
+                op1=ALU.min,
+                accum_out=negmax[:],
+            )
             live["sp", i] = (sp, negmax)
 
         def expo(i):
@@ -224,47 +203,25 @@ def tile_single_head_split_window_attention_1d_kernel(
                 in_=sp[:],
                 func=ACT.Exp,
                 bias=negmax[:],
-                scale=(1.0 if a in VPATH else -1.0),
+                scale=-1.0,
                 accum_out=live["rowsum", u][:, a : a + 1],
             )
 
-        def teh(i):
-            j, a = i // 2, i % 2
-            if a == 0:
-                live["eT", j] = ps_e.tile([P, 2, 4, P], BF16, name="eT")
-            for t in range(4):
-                nc.tensor.transpose(
-                    out=live["eT", j][:, a, t, :],
-                    in_=live["e", j][:, a, P * t : P * t + P],
-                    identity=ident[:],
-                )
+        def te(j):
+            eT = ps_e.tile([P, 2, 4, P], BF16, name="eT")
+            for a in range(2):
+                for t in range(4):
+                    nc.tensor.transpose(
+                        out=eT[:, a, t, :],
+                        in_=live["e", j][:, a, P * t : P * t + P],
+                        identity=ident[:],
+                    )
+            live["eT", j] = eT
 
         def eve(j):
-            eT = live["eT", j]
-            if j in DIRECT:
-                g_sb = work.tile([P, 2, P, 4], BF16, name="g_sb", align_bytes=64)
-                if j % 2 == 0:
-                    nc.scalar.copy(out=g_sb[:], in_=eT[:].rearrange("p a t q -> p a q t"))
-                else:
-                    nc.vector.tensor_copy(out=g_sb[:], in_=eT[:].rearrange("p a t q -> p a q t"))
-                live["g", j] = g_sb
-            else:
-                x_sb = work.tile([P, 2, 4, P], BF16, name="x_sb")
-                nc.scalar.copy(out=x_sb[:], in_=eT[:])
-                live["x", j] = x_sb
-
-        def gi(j):
-            if j not in DIRECT:
-                g_sb = work.tile([P, 2, P, 4], BF16, name="g_sb", align_bytes=64)
-                nc.gpsimd.tensor_scalar(
-                    out=g_sb[:],
-                    in0=live["x", j][:].rearrange("p a t q -> p a q t"),
-                    scalar1=1.0,
-                    scalar2=0.0,
-                    op0=ALU.mult,
-                    op1=ALU.add,
-                )
-                live["g", j] = g_sb
+            g_sb = work.tile([P, 2, P, 4], BF16, name="g_sb", align_bytes=64)
+            nc.scalar.copy(out=g_sb[:], in_=live["eT", j][:].rearrange("p a t q -> p a q t"))
+            live["g", j] = g_sb
 
         def qnt(j):
             u, b = j // 2, j % 2
@@ -311,47 +268,49 @@ def tile_single_head_split_window_attention_1d_kernel(
                 nc.sync.dma_start(out=o_v[:, g, :, :], in_=o_sb[:, 2 * hh : 2 * hh + 2, :])
 
         tqk(0)
-        evqk(0, True)
+        evqk(0)
         bias_t(0, 0, 1, False)
         bias_t(0, 1, 1, False)
-        bias_t(0, 2, 1, True)
         bias_ev(0, 0, 1, True)
         bias_ev(0, 1, 1, False)
-        bias_ev(0, 2, 1, True)
 
         for s in range(PAIRS + 7):
-            for a in range(2):
-                if s < PAIRS:
-                    score(2 * s + a)
-                if 0 <= s - 2 < PAIRS:
-                    teh(2 * (s - 2) + a)
-            if s % 2 == 0 and 0 <= (s - 6) // 2 < UNITS:
-                mxu((s - 6) // 2)
+            m = s - 1
+            unit_out = (s - 6) // 2 if s % 2 == 0 else -1
+            if s in (3, 4):
+                bias_t(1, 2 * (s - 3), 2, True)
+            if s < PAIRS:
+                qk(2 * s)
+                qk(2 * s + 1)
+                addbias(2 * s)
+                addbias(2 * s + 1)
+            if 0 <= unit_out < UNITS:
+                mxu(unit_out)
             if s % 2 == 0 and s // 2 + 1 < UNITS:
                 tqk(s // 2 + 1)
-            if 0 <= s - 1 < PAIRS:
-                rowmax(2 * (s - 1))
-                rowmax(2 * (s - 1) + 1)
-            if 0 <= s - 4 < PAIRS:
-                qnt(s - 4)
-            if s % 2 == 0 and 0 <= (s - 2) // 2 < UNITS:
-                vquant((s - 2) // 2)
-            if s % 2 == 0 and 0 <= (s - 6) // 2 < UNITS:
-                outu((s - 6) // 2)
-            if 0 <= s - 1 < PAIRS:
-                expo(2 * (s - 1))
-                expo(2 * (s - 1) + 1)
             if 0 <= s - 2 < PAIRS:
-                eve(s - 2)
-            if s % 2 == 0 and s // 2 + 1 < UNITS:
-                evqk(s // 2 + 1, False)
-            if 0 <= s - 2 < PAIRS:
-                gi(s - 2)
-            if s % 2 == 1 and s // 2 < UNITS:
-                vprep(s // 2)
-            if s == 2:
-                bias_t(1, 0, 2, True)
-                bias_ev(1, 0, 2, True)
-            if s == 4:
-                bias_t(1, 2, 1, True)
-                bias_ev(1, 2, 1, True)
+                te(s - 2)
+            if s == 0:
+                bias_t(0, 2, 2, True)
+            if 0 <= m < PAIRS:
+                rowmax(2 * m)
+                rowmax(2 * m + 1)
+            if m >= 0 and m % 2 == 0 and m // 2 + 1 < UNITS:
+                evqk(m // 2 + 1)
+            if m >= 0 and m % 2 == 0 and m // 2 < UNITS:
+                vprep(m // 2)
+            if 0 <= m - 3 < PAIRS:
+                qnt(m - 3)
+            if m >= 0 and m % 2 == 0 and m // 2 < UNITS:
+                vquant(m // 2)
+            if 0 <= unit_out < UNITS:
+                outu(unit_out)
+            if s in (3, 4):
+                bias_ev(1, 2 * (s - 3), 2, True)
+            if s == 0:
+                bias_ev(0, 2, 2, False)
+            if 0 <= m < PAIRS:
+                expo(2 * m)
+                expo(2 * m + 1)
+            if 0 <= m - 1 < PAIRS:
+                eve(m - 1)

@@ -7,7 +7,6 @@ BF16 = mybir.dt.bfloat16
 F32 = mybir.dt.float32
 U32 = mybir.dt.uint32
 U8 = mybir.dt.uint8
-I32 = mybir.dt.int32
 FP8X4 = mybir.dt.float8_e4m3fn_x4
 ALU = mybir.AluOpType
 ACT = mybir.ActivationFunctionType
@@ -139,9 +138,13 @@ def tile_single_head_split_window_attention_1d_kernel(
 
         def vprep(u):
             gv = work.tile([P, C, 4], BF16, name="gv", align_bytes=64)
-            nc.vector.tensor_copy(
-                out=gv[:].rearrange("p (c i) t -> p c t i", i=4),
-                in_=v_sb[u][:].rearrange("p t (c i) -> p c t i", i=4),
+            nc.gpsimd.tensor_scalar(
+                out=gv[:],
+                in0=v_sb[u][:].rearrange("p t c -> p c t"),
+                scalar1=1.0,
+                scalar2=0.0,
+                op0=ALU.mult,
+                op1=ALU.add,
             )
             live["gv", u] = gv
 
@@ -218,10 +221,34 @@ def tile_single_head_split_window_attention_1d_kernel(
                     )
             live["eT", j] = eT
 
-        def eve(j):
+        def eve(j, on_vector):
             g_sb = work.tile([P, 2, P, 4], BF16, name="g_sb", align_bytes=64)
-            nc.scalar.copy(out=g_sb[:], in_=live["eT", j][:].rearrange("p a t q -> p a q t"))
+            if on_vector:
+                nc.vector.tensor_copy(
+                    out=g_sb[:], in_=live["eT", j][:].rearrange("p a t q -> p a q t")
+                )
+            else:
+                nc.scalar.copy(out=g_sb[:], in_=live["eT", j][:].rearrange("p a t q -> p a q t"))
             live["g", j] = g_sb
+
+        def te_one(i):
+            eT1 = ps_s.tile([P, 4, P], BF16, name="eT1", tag="s_ps")
+            for t in range(4):
+                nc.tensor.transpose(
+                    out=eT1[:, t, :],
+                    in_=live["e", i // 2][:, i % 2, P * t : P * t + P],
+                    identity=ident[:],
+                )
+            live["eT1", i] = eT1
+
+        def eve_one(i, on_vector):
+            if i % 2 == 0:
+                live["g", i // 2] = work.tile([P, 2, P, 4], BF16, name="g_sb", align_bytes=64)
+            dst = live["g", i // 2][:, i % 2, :, :]
+            if on_vector:
+                nc.vector.tensor_copy(out=dst, in_=live["eT1", i][:].rearrange("p t q -> p q t"))
+            else:
+                nc.scalar.copy(out=dst, in_=live["eT1", i][:].rearrange("p t q -> p q t"))
 
         def qnt(j):
             u, b = j // 2, j % 2
@@ -237,9 +264,12 @@ def tile_single_head_split_window_attention_1d_kernel(
                 in_=live["g", j][:].rearrange("p a q t -> p (a q t)"),
             )
 
-        def mxu(u):
+        def mxu(u, spare):
             e_codes, e_scales = live["c", u]
-            o_ps = ps_o.tile([P, 4, C], F32, name="o_ps")
+            if spare:
+                o_ps = ps_s.tile([P, 4, C], F32, name="o_ps", tag="s_ps")
+            else:
+                o_ps = ps_o.tile([P, 4, C], F32, name="o_ps")
             for a in range(4):
                 nc.tensor.matmul_mx(
                     out=o_ps[:, a, :],
@@ -252,17 +282,30 @@ def tile_single_head_split_window_attention_1d_kernel(
                 )
             live["o", u] = o_ps
 
-        def outu(u):
-            r, n = u % ROWS, u // ROWS
+        def recip(u):
             rinv = stat.tile([P, 4], F32, name="rinv")
             nc.vector.reciprocal(out=rinv[:], in_=live["rowsum", u][:])
+            live["rinv", u] = rinv
+
+        def outu(u, on_vector):
+            r, n = u % ROWS, u // ROWS
+            rinv = live["rinv", u]
             o_sb = work.tile([P, 4, C], F32, name="o_sb")
-            nc.vector.tensor_tensor(
-                out=o_sb[:],
-                in0=live["o", u][:],
-                in1=rinv[:].unsqueeze(2).to_broadcast([P, 4, C]),
-                op=ALU.mult,
-            )
+            if on_vector:
+                nc.vector.tensor_tensor(
+                    out=o_sb[:],
+                    in0=live["o", u][:],
+                    in1=rinv[:].unsqueeze(2).to_broadcast([P, 4, C]),
+                    op=ALU.mult,
+                )
+            else:
+                for a in range(4):
+                    nc.scalar.activation(
+                        out=o_sb[:, a, :],
+                        in_=live["o", u][:, a, :],
+                        func=ACT.Copy,
+                        scale=rinv[:, a : a + 1],
+                    )
             for hh in range(2):
                 g = 4 * r + (1 + 2 * n + hh) % 4
                 nc.sync.dma_start(out=o_v[:, g, :, :], in_=o_sb[:, 2 * hh : 2 * hh + 2, :])
@@ -274,43 +317,81 @@ def tile_single_head_split_window_attention_1d_kernel(
         bias_ev(0, 0, 1, True)
         bias_ev(0, 1, 1, False)
 
-        for s in range(PAIRS + 7):
+        for s in range(PAIRS - 1):
             m = s - 1
             unit_out = (s - 6) // 2 if s % 2 == 0 else -1
             if s in (3, 4):
                 bias_t(1, 2 * (s - 3), 2, True)
-            if s < PAIRS:
-                qk(2 * s)
-                qk(2 * s + 1)
-                addbias(2 * s)
-                addbias(2 * s + 1)
-            if 0 <= unit_out < UNITS:
-                mxu(unit_out)
+            qk(2 * s)
+            qk(2 * s + 1)
+            addbias(2 * s)
+            addbias(2 * s + 1)
+            if unit_out >= 0:
+                mxu(unit_out, False)
             if s % 2 == 0 and s // 2 + 1 < UNITS:
                 tqk(s // 2 + 1)
-            if 0 <= s - 2 < PAIRS:
+            if s >= 2:
                 te(s - 2)
             if s == 0:
                 bias_t(0, 2, 2, True)
-            if 0 <= m < PAIRS:
+            if m >= 0:
                 rowmax(2 * m)
                 rowmax(2 * m + 1)
-            if m >= 0 and m % 2 == 0 and m // 2 + 1 < UNITS:
+            if m >= 0 and m % 2 == 0:
                 evqk(m // 2 + 1)
-            if m >= 0 and m % 2 == 0 and m // 2 < UNITS:
-                vprep(m // 2)
-            if 0 <= m - 3 < PAIRS:
+            if m >= 3:
                 qnt(m - 3)
-            if m >= 0 and m % 2 == 0 and m // 2 < UNITS:
+            if m >= 0 and m % 2 == 0:
                 vquant(m // 2)
-            if 0 <= unit_out < UNITS:
-                outu(unit_out)
+            if unit_out >= 0:
+                recip(unit_out)
+                outu(unit_out, True)
             if s in (3, 4):
                 bias_ev(1, 2 * (s - 3), 2, True)
             if s == 0:
                 bias_ev(0, 2, 2, False)
-            if 0 <= m < PAIRS:
+            if m >= 0:
                 expo(2 * m)
                 expo(2 * m + 1)
-            if 0 <= m - 1 < PAIRS:
-                eve(m - 1)
+            if m >= 1:
+                eve(m - 1, False)
+            if s % 2 == 0:
+                vprep(s // 2)
+
+        qk(30)
+        qk(31)
+        addbias(30)
+        addbias(31)
+        te(13)
+        rowmax(28)
+        rowmax(29)
+        qnt(11)
+        vquant(7)
+        expo(28)
+        expo(29)
+
+        mxu(5, False)
+        te(14)
+        rowmax(30)
+        rowmax(31)
+        expo(30)
+        expo(31)
+        te_one(30)
+        te_one(31)
+        eve(13, True)
+        qnt(12)
+        recip(5)
+        outu(5, True)
+        qnt(13)
+        eve_one(30, True)
+        eve(14, False)
+        eve_one(31, False)
+
+        mxu(6, False)
+        recip(6)
+        qnt(14)
+        qnt(15)
+        recip(7)
+        outu(6, False)
+        mxu(7, True)
+        outu(7, True)

@@ -328,12 +328,12 @@ def tile_single_head_split_window_attention_1d_kernel(
             addbias(2 * s + 1)
             if unit_out >= 0:
                 mxu(unit_out, False)
+            if s == 0:
+                bias_t(0, 2, 2, True)
             if s % 2 == 0 and s // 2 + 1 < UNITS:
                 tqk(s // 2 + 1)
             if s >= 2:
                 te(s - 2)
-            if s == 0:
-                bias_t(0, 2, 2, True)
             if m >= 0:
                 rowmax(2 * m)
                 rowmax(2 * m + 1)

@@ -92,6 +92,12 @@ def tile_single_head_split_window_attention_1d_kernel(
         warm2 = const.tile([P, 1], F32, name="warm2")
         nc.scalar.activation(out=warm2[:], in_=warm[:], func=ACT.Exp)
 
+        zeros = const.tile([P, WIN], BF16, name="zeros")
+        nc.vector.memset(zeros[:], 0.0)
+        for d in range(3):
+            z_ps = ps_s.tile([P, WIN], F32, name="z_ps", tag="s_ps")
+            nc.tensor.matmul(out=z_ps[:], lhsT=ident[:], rhs=zeros[:], start=True, stop=True)
+
         bp = [const.tile([P, 4, 4, P], F32, name="bp%d" % n) for n in range(NWIN)]
         v_codes = [const.tile([P, C], U32, name="v_codes%d" % u, align_bytes=64) for u in range(UNITS)]
         v_scales = [const.tile([P, C], U8, name="v_scales%d" % u, align_bytes=64) for u in range(UNITS)]

from contextlib import ExitStack

import concourse.mybir as mybir
from concourse.masks import make_identity

BF16 = mybir.dt.bfloat16
F32 = mybir.dt.float32
U32 = mybir.dt.uint32
U8 = mybir.dt.uint8
FP8X4 = mybir.dt.float8_e4m3fn_x4
ALU = mybir.AluOpType
ACT = mybir.ActivationFunctionType

P = 128
C = 128
ROWS = 4
WIN = 512
NWIN = 2
UNITS = ROWS * NWIN
PAIRS = 2 * UNITS
FLOPS = 2 * UNITS * 2 * WIN * WIN * C


def tile_single_head_split_window_attention_1d_kernel(
    tc, q, k, v, attn_mask, h, w, num_splits, out
):
    nc = tc.nc
    assert h == 2 and w == 1024 and num_splits == 2
    scale = 1.0 / (C ** 0.5)

    q_v = q.flatten_outer_dims().rearrange("(g p j) c -> p g j c", p=P, j=2)
    k_v = k.flatten_outer_dims().rearrange("(t p) c -> p t c", p=P)
    v_v = v.flatten_outer_dims().rearrange("(t p) c -> p t c", p=P)
    b_v = attn_mask.rearrange("n (h p j) k -> p n h j k", p=P, j=2)
    o_v = out.flatten_outer_dims().rearrange("(g p j) c -> p g j c", p=P, j=2)

    with ExitStack() as ctx:
        const = ctx.enter_context(tc.tile_pool(name="const", bufs=1))
        work = ctx.enter_context(tc.tile_pool(name="work", bufs=4))
        stat = ctx.enter_context(tc.tile_pool(name="stat", bufs=8))
        ps_t = ctx.enter_context(tc.psum_pool(name="ps_t", bufs=1))
        ps_s = ctx.enter_context(tc.psum_pool(name="ps_s", bufs=4))
        ps_e = ctx.enter_context(tc.psum_pool(name="ps_e", bufs=2))
        ps_o = ctx.enter_context(tc.psum_pool(name="ps_o", bufs=1))
        ctx.enter_context(tc.manual_schedule())

        k_sb = [const.tile([P, 4, C], BF16, name="k_sb%d" % u) for u in range(UNITS)]
        q_sb = [const.tile([P, 2, 2, C], BF16, name="q_sb%d" % u) for u in range(UNITS)]
        v_sb = [const.tile([P, 4, C], BF16, name="v_sb%d" % u) for u in range(UNITS)]
        b_sb = [
            [const.tile([P, 2, WIN], BF16, name="b_sb%d%d" % (n, hh)) for hh in range(2)]
            for n in range(NWIN)
        ]

        def load_tiles(dst, src, u):
            r, n = u % ROWS, u // ROWS
            if n == 0:
                nc.sync.dma_start(out=dst[:], in_=src[:, 8 * r + 2 : 8 * r + 6, :])
            else:
                nc.sync.dma_start(out=dst[:, 0:2, :], in_=src[:, 8 * r + 6 : 8 * r + 8, :])
                nc.sync.dma_start(out=dst[:, 2:4, :], in_=src[:, 8 * r : 8 * r + 2, :])

        def load_q(u):
            r, n = u % ROWS, u // ROWS
            if n == 0:
                nc.sync.dma_start(out=q_sb[u][:], in_=q_v[:, 4 * r + 1 : 4 * r + 3, :, :])
            else:
                nc.sync.dma_start(out=q_sb[u][:, 0], in_=q_v[:, 4 * r + 3, :, :])
                nc.sync.dma_start(out=q_sb[u][:, 1], in_=q_v[:, 4 * r, :, :])

        def load_bias(n):
            for hh in range(2):
                nc.sync.dma_start(out=b_sb[n][hh][:], in_=b_v[:, n, hh])

        for u in range(UNITS):
            load_tiles(k_sb[u], k_v, u)
            load_q(u)
            if u == 0:
                load_bias(0)
            else:
                load_tiles(v_sb[u - 1], v_v, u - 1)
            if u == 1:
                load_bias(1)
        load_tiles(v_sb[UNITS - 1], v_v, UNITS - 1)

        ident = const.tile([P, P], BF16, name="ident")
        make_identity(nc, ident[:])
        ident_f = const.tile([P, P], F32, name="ident_f")
        make_identity(nc, ident_f[:])
        warm = const.tile([P, 1], F32, name="warm")
        nc.vector.memset(warm[:], 0.0)
        warm2 = const.tile([P, 1], F32, name="warm2")
        nc.scalar.activation(out=warm2[:], in_=warm[:], func=ACT.Exp)

        zeros = const.tile([P, WIN], BF16, name="zeros")
        nc.vector.memset(zeros[:], 0.0)
        for d in range(3):
            z_ps = ps_s.tile([P, WIN], F32, name="z_ps", tag="s_ps")
            nc.tensor.matmul(out=z_ps[:], lhsT=ident[:], rhs=zeros[:], start=True, stop=True)

        bp = [const.tile([P, 4, 4, P], F32, name="bp%d" % n) for n in range(NWIN)]
        v_codes = [const.tile([P, C], U32, name="v_codes%d" % u, align_bytes=64) for u in range(UNITS)]
        v_scales = [const.tile([P, C], U8, name="v_scales%d" % u, align_bytes=64) for u in range(UNITS)]

        live = {}

        def bias_t(n, a0, na, spare):
            if spare:
                bT = ps_o.tile([P, na, 4, P], BF16, name="bT", tag="o_ps")
            else:
                bT = ps_e.tile([P, na, 4, P], BF16, name="bT", tag="eT")
            for a in range(na):
                for t in range(4):
                    nc.tensor.transpose(
                        out=bT[:, a, t, :],
                        in_=b_sb[n][(a0 + a) // 2][:, (a0 + a) % 2, P * t : P * t + P],
                        identity=ident[:],
                    )
            live["bT", n, a0] = bT

        def bias_ev(n, a0, na, on_vector):
            bT = live["bT", n, a0]
            if on_vector:
                nc.vector.tensor_scalar_mul(
                    out=bp[n][:, a0 : a0 + na, :, :], in0=bT[:], scalar1=C ** 0.5
                )
            else:
                nc.scalar.mul(out=bp[n][:, a0 : a0 + na, :, :], in_=bT[:], mul=C ** 0.5)

        def tqk(u):
            t_ps = ps_t.tile([P, 8, P], BF16, name="t_ps")
            for t in range(4):
                nc.tensor.transpose(out=t_ps[:, t, :], in_=k_sb[u][:, t, :], identity=ident[:])
            for a in range(4):
                nc.tensor.transpose(
                    out=t_ps[:, 4 + a, :], in_=q_sb[u][:, a // 2, a % 2, :], identity=ident[:]
                )
            live["t_ps", u] = t_ps

        def evqk(u):
            qkT = work.tile([P, 8, P], BF16, name="qkT")
            nc.vector.tensor_copy(out=qkT[:], in_=live["t_ps", u][:])
            live["qkT", u] = qkT

        def vprep(u):
            gv = work.tile([P, C, 4], BF16, name="gv", align_bytes=64)
            nc.gpsimd.tensor_scalar(
                out=gv[:],
                in0=v_sb[u][:].rearrange("p t c -> p c t"),
                scalar1=1.0,
                scalar2=0.0,
                op0=ALU.mult,
                op1=ALU.add,
            )
            live["gv", u] = gv

        def vquant(u):
            nc.vector.quantize_mx(
                out=v_codes[u][:].bitcast(FP8X4),
                scales=v_scales[u][:],
                in_=live["gv", u][:].rearrange("p c t -> p (c t)"),
            )

        def qk(i):
            u, a = i // 4, i % 4
            qkT = live["qkT", u]
            s_ps = ps_s.tile([P, WIN], F32, name="s_ps")
            nc.tensor.matmul(
                out=s_ps[:],
                lhsT=qkT[:, 4 + a, :],
                rhs=qkT[:, 0:4, :].rearrange("p t k -> p (t k)"),
                start=True,
                stop=False,
            )
            live["s_ps", i] = s_ps

        def addbias(i):
            u, a = i // 4, i % 4
            for t in range(4):
                nc.tensor.matmul(
                    out=live["s_ps", i][:, P * t : P * t + P],
                    lhsT=bp[u // ROWS][:, a, t, :],
                    rhs=ident_f[:],
                    is_transpose=True,
                    start=False,
                    stop=(t == 3),
                )

        def rowmax(i):
            sp = work.tile([P, WIN], F32, name="sp")
            negmax = stat.tile([P, 1], F32, name="negmax")
            nc.vector.tensor_scalar(
                out=sp[:],
                in0=live["s_ps", i][:],
                scalar1=-scale,
                scalar2=None,
                op0=ALU.mult,
                op1=ALU.min,
                accum_out=negmax[:],
            )
            live["sp", i] = (sp, negmax)

        def expo(i):
            u, a = i // 4, i % 4
            if a == 0:
                live["rowsum", u] = stat.tile([P, 4], F32, name="rowsum")
            if a % 2 == 0:
                live["e", i // 2] = work.tile([P, 2, WIN], BF16, name="e_sb")
            sp, negmax = live["sp", i]
            nc.scalar.activation(
                out=live["e", i // 2][:, a % 2, :],
                in_=sp[:],
                func=ACT.Exp,
                bias=negmax[:],
                scale=-1.0,
                accum_out=live["rowsum", u][:, a : a + 1],
            )

        def te(j):
            eT = ps_e.tile([P, 2, 4, P], BF16, name="eT")
            for a in range(2):
                for t in range(4):
                    nc.tensor.transpose(
                        out=eT[:, a, t, :],
                        in_=live["e", j][:, a, P * t : P * t + P],
                        identity=ident[:],
                    )
            live["eT", j] = eT

        def eve(j, on_vector):
            g_sb = work.tile([P, 2, P, 4], BF16, name="g_sb", align_bytes=64)
            if on_vector:
                nc.vector.tensor_copy(
                    out=g_sb[:], in_=live["eT", j][:].rearrange("p a t q -> p a q t")
                )
            else:
                nc.scalar.copy(out=g_sb[:], in_=live["eT", j][:].rearrange("p a t q -> p a q t"))
            live["g", j] = g_sb

        def te_one(i):
            eT1 = ps_s.tile([P, 4, P], BF16, name="eT1", tag="s_ps")
            for t in range(4):
                nc.tensor.transpose(
                    out=eT1[:, t, :],
                    in_=live["e", i // 2][:, i % 2, P * t : P * t + P],
                    identity=ident[:],
                )
            live["eT1", i] = eT1

        def eve_one(i, on_vector):
            if i % 2 == 0:
                live["g", i // 2] = work.tile([P, 2, P, 4], BF16, name="g_sb", align_bytes=64)
            dst = live["g", i // 2][:, i % 2, :, :]
            if on_vector:
                nc.vector.tensor_copy(out=dst, in_=live["eT1", i][:].rearrange("p t q -> p q t"))
            else:
                nc.scalar.copy(out=dst, in_=live["eT1", i][:].rearrange("p t q -> p q t"))

        def qnt(j):
            u, b = j // 2, j % 2
            if b == 0:
                live["c", u] = (
                    work.tile([P, 4 * P], U32, name="e_codes", align_bytes=64),
                    work.tile([P, 4 * P], U8, name="e_scales", align_bytes=64),
                )
            e_codes, e_scales = live["c", u]
            nc.vector.quantize_mx(
                out=e_codes[:, 2 * P * b : 2 * P * b + 2 * P].bitcast(FP8X4),
                scales=e_scales[:, 2 * P * b : 2 * P * b + 2 * P],
                in_=live["g", j][:].rearrange("p a q t -> p (a q t)"),
            )

        def mxu(u, spare):
            e_codes, e_scales = live["c", u]
            if spare:
                o_ps = ps_s.tile([P, 4, C], F32, name="o_ps", tag="s_ps")
            else:
                o_ps = ps_o.tile([P, 4, C], F32, name="o_ps")
            for a in range(4):
                nc.tensor.matmul_mx(
                    out=o_ps[:, a, :],
                    lhsT=e_codes[:, P * a : P * a + P].bitcast(FP8X4),
                    lhsT_scale=e_scales[:, P * a : P * a + P],
                    rhs=v_codes[u][:].bitcast(FP8X4),
                    rhs_scale=v_scales[u][:],
                    start=True,
                    stop=True,
                )
            live["o", u] = o_ps

        def recip(u):
            rinv = stat.tile([P, 4], F32, name="rinv")
            nc.vector.reciprocal(out=rinv[:], in_=live["rowsum", u][:])
            live["rinv", u] = rinv

        def outu(u, on_vector):
            r, n = u % ROWS, u // ROWS
            rinv = live["rinv", u]
            o_sb = work.tile([P, 4, C], F32, name="o_sb")
            if on_vector:
                nc.vector.tensor_tensor(
                    out=o_sb[:],
                    in0=live["o", u][:],
                    in1=rinv[:].unsqueeze(2).to_broadcast([P, 4, C]),
                    op=ALU.mult,
                )
            else:
                for a in range(4):
                    nc.scalar.activation(
                        out=o_sb[:, a, :],
                        in_=live["o", u][:, a, :],
                        func=ACT.Copy,
                        scale=rinv[:, a : a + 1],
                    )
            for hh in range(2):
                g = 4 * r + (1 + 2 * n + hh) % 4
                nc.sync.dma_start(out=o_v[:, g, :, :], in_=o_sb[:, 2 * hh : 2 * hh + 2, :])

        tqk(0)
        evqk(0)
        bias_t(0, 0, 1, False)
        bias_t(0, 1, 1, False)
        bias_ev(0, 0, 1, True)
        bias_ev(0, 1, 1, False)

        for s in range(PAIRS - 1):
            m = s - 1
            unit_out = (s - 6) // 2 if s % 2 == 0 else -1
            if s in (3, 4):
                bias_t(1, 2 * (s - 3), 2, True)
            qk(2 * s)
            qk(2 * s + 1)
            addbias(2 * s)
            addbias(2 * s + 1)
            if unit_out >= 0:
                mxu(unit_out, False)
            if s == 0:
                bias_t(0, 2, 2, True)
            if s % 2 == 0 and s // 2 + 1 < UNITS:
                tqk(s // 2 + 1)
            if s >= 2:
                te(s - 2)
            if m >= 0:
                rowmax(2 * m)
                rowmax(2 * m + 1)
            if m >= 0 and m % 2 == 0:
                evqk(m // 2 + 1)
            if m >= 3:
                qnt(m - 3)
            if m >= 0 and m % 2 == 0:
                vquant(m // 2)
            if unit_out >= 0:
                recip(unit_out)
                outu(unit_out, True)
            if s in (3, 4):
                bias_ev(1, 2 * (s - 3), 2, True)
            if s == 0:
                bias_ev(0, 2, 2, False)
            if m >= 0:
                expo(2 * m)
                expo(2 * m + 1)
            if m >= 1:
                eve(m - 1, False)
            if s % 2 == 0:
                vprep(s // 2)

        qk(30)
        qk(31)
        addbias(30)
        addbias(31)
        te(13)
        rowmax(28)
        rowmax(29)
        qnt(11)
        vquant(7)
        expo(28)
        expo(29)

        mxu(5, False)
        te(14)
        rowmax(30)
        rowmax(31)
        expo(30)
        expo(31)
        te_one(30)
        te_one(31)
        eve(13, True)
        qnt(12)
        recip(5)
        outu(5, True)
        qnt(13)
        eve_one(30, True)
        eve(14, False)
        eve_one(31, False)

        mxu(6, False)
        recip(6)
        qnt(14)
        qnt(15)
        recip(7)
        outu(6, False)
        mxu(7, True)
        outu(7, True)
